import numpy as np
import ml_dtypes


def mxq(x, axis, fmt="e4m3"):
    dtype, down = {"e4m3": (ml_dtypes.float8_e4m3fn, 7), "e5m2": (ml_dtypes.float8_e5m2, 14)}[fmt]
    v = np.moveaxis(np.asarray(x, np.float32).astype(ml_dtypes.bfloat16).astype(np.float64), axis, -1)
    blocks = v.reshape(v.shape[:-1] + (-1, 32))
    amax = np.abs(blocks).max(-1, keepdims=True)
    byte = np.maximum(np.where(amax > 0, np.frexp(amax)[1] - 1 + 127, 0) - down, 1)
    scale = np.exp2(byte - 127.0)
    codes = (blocks / scale).astype(np.float32).astype(dtype).astype(np.float64)
    return np.moveaxis((codes * scale).reshape(v.shape), -1, axis)


WIDE = False


def mx_kscale(k):
    if not WIDE:
        return np.ones(k)
    levels = np.array([20, -20, 10, -10, 0])
    if k % 512:
        return np.exp2(np.random.permutation(np.resize(levels, k // 32))).repeat(32)
    a = np.empty((k // 512, 16))
    for p in range(k // 512):
        a[p, :8] = np.random.permutation(np.resize(levels, 8))
        for g in range(8):
            far = levels[np.abs(levels - a[p, g]) >= 10]
            a[p, g + 8] = far[np.random.randint(len(far))]
    return np.exp2(a.ravel()).repeat(32)


BF16 = ml_dtypes.bfloat16


def bf(x):
    return np.asarray(x, np.float32).astype(BF16)


def f64(x):
    return np.asarray(x).astype(np.float64)


B, T, HP, WP, NH, D, DFF = 8, 7, 3, 3, 16, 512, 2048
HW = HP * WP
N = 1 + HW * T


def setup_inputs():
    u = mx_kscale(D)
    c = np.random.standard_normal((B * T, 1 + HW, D)) * 1.5 / np.sqrt(1 + HW)
    c[:, 0, :] *= 5.0
    xr = np.random.standard_normal((B, N, D)) * 1.1
    w = np.random.standard_normal((D, D)) / np.sqrt(D) / u[None, :]
    b = 0.1 * np.random.standard_normal(D)
    g = np.random.standard_normal((B, N, D)) * np.exp2(np.random.randint(-12, 1, (B, N, 1))) * 16.0 * u
    return {"ctx_s": bf(c),
            "x_res": bf(xr),
            "s_out_w": bf(w),
            "s_out_b": bf(b),
            "grad_out": bf(g)}


def reference(ctx_s, x_res, s_out_w, s_out_b, grad_out):
    g2 = f64(grad_out).reshape(B * N, D)
    h = mxq(g2, 1, "e5m2") @ mxq(f64(s_out_w), 1, "e4m3").T
    h = h.reshape(B, N, D)
    cls = np.broadcast_to(h[:, :1, :] / T, (B, T, D)).reshape(B * T, 1, D)
    pat = h[:, 1:, :].reshape(B, HW, T, D).swapaxes(1, 2).reshape(B * T, HW, D)
    return np.concatenate([cls, pat], axis=1)

@@ -1,0 +1,164 @@
+from contextlib import ExitStack
+
+import concourse.mybir as mybir
+from concourse.masks import make_identity
+
+BF16 = mybir.dt.bfloat16
+F32 = mybir.dt.float32
+U32 = mybir.dt.uint32
+U8 = mybir.dt.uint8
+E5M2_X4 = mybir.dt.float8_e5m2_x4
+E4M3_X4 = mybir.dt.float8_e4m3fn_x4
+
+P = 128
+SAMPLES = 8
+FRAMES = 7
+POSITIONS = 10
+TOKENS = 64
+D = 512
+
+HALVES = 2
+PASSES = POSITIONS // HALVES
+USED = SAMPLES * FRAMES * HALVES
+TILE_SAMPLES = P // TOKENS
+ROW_TILES = D // P
+SLOTS = TILE_SAMPLES * FRAMES * HALVES
+FULL_PASSES = PASSES - 1
+FULL_SORTED = FULL_PASSES * SLOTS
+TILE_SEQUENCES = TILE_SAMPLES * FRAMES
+WORD_PLANES = 2
+BANK_WORDS = 512
+
+FLOPS = 2 * SAMPLES * TOKENS * D * D
+BYTES = 2 * (SAMPLES * TOKENS * D + D * D) + 4 * SAMPLES * FRAMES * POSITIONS * D
+
+
+def tile_timesformerlayer_pc_s_kernel(tc, ctx_s, x_res, s_out_w, s_out_b, grad_out, out):
+    nc = tc.nc
+    with ExitStack() as ctx:
+        consts = ctx.enter_context(tc.tile_pool(name="consts", bufs=1))
+        loaded = ctx.enter_context(tc.tile_pool(name="loaded", bufs=2 * ROW_TILES))
+        operands = ctx.enter_context(tc.tile_pool(name="operands", bufs=1))
+        results = ctx.enter_context(tc.tile_pool(name="results", bufs=PASSES))
+        flip_banks = ctx.enter_context(tc.psum_pool(name="flip_banks", bufs=4))
+        acc_banks = ctx.enter_context(tc.psum_pool(name="acc_banks", bufs=4))
+
+        grad_rows = grad_out.rearrange("b n k -> (b n) k")
+        grad_tiles = []
+        weight_tiles = []
+        for source, tiles in ((grad_rows, grad_tiles), (s_out_w, weight_tiles)):
+            for r in range(ROW_TILES):
+                rows = loaded.tile([P, D], BF16)
+                nc.sync.dma_start(out=rows[:], in_=source[r * P : (r + 1) * P, :])
+                tiles.append(rows)
+
+        ident = consts.tile([P, P], F32)
+        make_identity(nc, ident[:])
+        sorter = consts.tile([P, P], F32)
+        full = sorter[:, 0:FULL_SORTED].rearrange(
+            "k (i l t h) -> k i l t h", i=FULL_PASSES, l=TILE_SAMPLES, t=FRAMES, h=HALVES
+        )
+        token = ident[:].rearrange("k (l n) -> k l n", l=TILE_SAMPLES)
+        for h in range(HALVES):
+            first = FRAMES * (PASSES * h + 1) - (FRAMES - 1)
+            nc.vector.tensor_copy(
+                out=full[:, :, :, :, h],
+                in_=token[:, :, first : first + FULL_PASSES * FRAMES].rearrange("k l (i t) -> k i l t", t=FRAMES),
+            )
+        first = FRAMES * PASSES - (FRAMES - 1)
+        nc.vector.tensor_copy(
+            out=sorter[:, FULL_SORTED : FULL_SORTED + TILE_SEQUENCES].rearrange("k (l t) -> k l t", t=FRAMES),
+            in_=token[:, :, first : first + FRAMES],
+        )
+        nc.vector.tensor_copy(out=sorter[:, FULL_SORTED + TILE_SEQUENCES : P], in_=token[:, :, 0])
+
+        grad_grouped = operands.tile([P, PASSES * P * 4], BF16, align_bytes=64)
+        grad_codes = operands.tile([P, PASSES * P], U32, align_bytes=64)
+        grad_scales = operands.tile([P, PASSES * P], U8, align_bytes=64)
+        weight_grouped = operands.tile([P, D * 4], BF16, align_bytes=64)
+        weight_codes = operands.tile([P, D], U32, align_bytes=64)
+        weight_scales = operands.tile([P, D], U8, align_bytes=64)
+        grad_words = grad_grouped[:].bitcast(F32).rearrange(
+            "k (i q u) -> k i q u", i=PASSES, q=P, u=WORD_PLANES
+        )
+        weight_words = weight_grouped[:].bitcast(F32).rearrange("k (c u) -> k c u", u=WORD_PLANES)
+        nc.vector.memset(grad_grouped[:].bitcast(F32), 0.0)
+
+        for r in range(ROW_TILES):
+            words = grad_tiles[r][:].bitcast(F32)
+            flipped = flip_banks.tile([P, WORD_PLANES, BANK_WORDS // WORD_PLANES], F32)
+            for u in range(WORD_PLANES):
+                nc.tensor.transpose(flipped[:, u, 0:P], words[:, u : D // 2 : WORD_PLANES], sorter[:])
+            mine = grad_words[:, :, r * SLOTS : (r + 1) * SLOTS, :]
+            moves = (
+                (
+                    mine[:, 1:PASSES, :, :],
+                    flipped[:, :, 0:FULL_SORTED].rearrange("k u (i c) -> k i c u", i=FULL_PASSES),
+                ),
+                (
+                    mine[:, 0, 1:SLOTS:HALVES, :],
+                    flipped[:, :, FULL_SORTED : FULL_SORTED + TILE_SEQUENCES].rearrange("k u c -> k c u"),
+                ),
+                (
+                    mine[:, 0, 0 : SLOTS : FRAMES * HALVES, :],
+                    flipped[:, :, FULL_SORTED + TILE_SEQUENCES : P].rearrange("k u c -> k c u"),
+                ),
+            )
+            for target, sorted_words in moves:
+                if r % 2 == 0:
+                    nc.vector.tensor_copy(out=target, in_=sorted_words)
+                else:
+                    nc.scalar.copy(out=target, in_=sorted_words)
+        for i in range(PASSES):
+            nc.vector.quantize_mx(
+                out=grad_codes[:, i * P : (i + 1) * P].bitcast(E5M2_X4),
+                scales=grad_scales[:, i * P : (i + 1) * P],
+                in_=grad_grouped[:, i * P * 4 : (i + 1) * P * 4],
+            )
+
+        for r in range(ROW_TILES):
+            words = weight_tiles[r][:].bitcast(F32)
+            flipped = flip_banks.tile([P, WORD_PLANES, BANK_WORDS // WORD_PLANES], F32)
+            for u in range(WORD_PLANES):
+                nc.tensor.transpose(flipped[:, u, 0:P], words[:, u : D // 2 : WORD_PLANES], ident[:])
+            nc.scalar.copy(
+                out=weight_words[:, r * P : (r + 1) * P, :],
+                in_=flipped[:, :, 0:P].rearrange("k u c -> k c u"),
+            )
+            nc.vector.quantize_mx(
+                out=weight_codes[:, r * P : (r + 1) * P].bitcast(E4M3_X4),
+                scales=weight_scales[:, r * P : (r + 1) * P],
+                in_=weight_grouped[:, r * P * 4 : (r + 1) * P * 4],
+            )
+
+        out_rows = out.rearrange("j s d -> (j s) d").rearrange("(q i) d -> q i d", i=PASSES)
+        class_rows_of_out = out.rearrange("(b t) s d -> b t s d", t=FRAMES)[:, :, 0, :]
+        for i in range(PASSES):
+            acc = acc_banks.tile([P, D], F32)
+            nc.tensor.matmul_mx(
+                out=acc[:],
+                lhsT=grad_codes[:, i * P : (i + 1) * P].bitcast(E5M2_X4),
+                lhsT_scale=grad_scales[:, i * P : (i + 1) * P],
+                rhs=weight_codes[:].bitcast(E4M3_X4),
+                rhs_scale=weight_scales[:],
+                start=True,
+                stop=True,
+            )
+            result = results.tile([P, D], F32)
+            if i == 0:
+                nc.vector.tensor_copy(out=result[:], in_=acc[:])
+                nc.sync.dma_start(out=out[:, PASSES, :], in_=result[1:USED:HALVES, :])
+                class_result = results.tile([P, D], F32)
+                nc.vector.tensor_scalar_mul(out=class_result[:], in0=acc[:], scalar1=1.0 / FRAMES)
+                nc.sync.dma_start(
+                    out=class_rows_of_out,
+                    in_=class_result[0 : USED : FRAMES * HALVES, :]
+                    .unsqueeze(1)
+                    .to_broadcast([SAMPLES, FRAMES, D]),
+                )
+            elif i % 2 == 0:
+                nc.vector.tensor_copy(out=result[:], in_=acc[:])
+                nc.sync.dma_start(out=out_rows[:, i, :], in_=result[0:USED, :])
+            else:
+                nc.scalar.copy(out=result[:], in_=acc[:])
+                nc.scalar.dma_start(out=out_rows[:, i, :], in_=result[0:USED, :])

@@ -9,156 +9,189 @@ U32 = mybir.dt.uint32
 U8 = mybir.dt.uint8
 E5M2_X4 = mybir.dt.float8_e5m2_x4
 E4M3_X4 = mybir.dt.float8_e4m3fn_x4
+ADD = mybir.AluOpType.add
+MULT = mybir.AluOpType.mult
+COPY = mybir.ActivationFunctionType.Copy
 
 P = 128
 SAMPLES = 8
 FRAMES = 7
 POSITIONS = 10
+PATCHES = 9
 TOKENS = 64
 D = 512
-
-HALVES = 2
-PASSES = POSITIONS // HALVES
-USED = SAMPLES * FRAMES * HALVES
+ROWS = SAMPLES * FRAMES * POSITIONS
 TILE_SAMPLES = P // TOKENS
-ROW_TILES = D // P
-SLOTS = TILE_SAMPLES * FRAMES * HALVES
-FULL_PASSES = PASSES - 1
-FULL_SORTED = FULL_PASSES * SLOTS
-TILE_SEQUENCES = TILE_SAMPLES * FRAMES
-WORD_PLANES = 2
-BANK_WORDS = 512
+GRAD_TILES = 4
+TILE_ROWS = TILE_SAMPLES * FRAMES * POSITIONS
+TILE_PATCHES = TILE_SAMPLES * FRAMES * PATCHES
+WEIGHT_LOADS = 2
+WEIGHT_RUN = 2
+WORDS = 2
+COLS = 576
+STARTS = (0, 128, 256, 384, 448)
 
 FLOPS = 2 * SAMPLES * TOKENS * D * D
-BYTES = 2 * (SAMPLES * TOKENS * D + D * D) + 4 * SAMPLES * FRAMES * POSITIONS * D
+BYTES = 2 * (SAMPLES * TOKENS * D + D * D) + 4 * ROWS * D
 
 
 def tile_timesformerlayer_pc_s_kernel(tc, ctx_s, x_res, s_out_w, s_out_b, grad_out, out):
     nc = tc.nc
     with ExitStack() as ctx:
         consts = ctx.enter_context(tc.tile_pool(name="consts", bufs=1))
-        loaded = ctx.enter_context(tc.tile_pool(name="loaded", bufs=2 * ROW_TILES))
+        loaded = ctx.enter_context(tc.tile_pool(name="loaded", bufs=4))
         operands = ctx.enter_context(tc.tile_pool(name="operands", bufs=1))
-        results = ctx.enter_context(tc.tile_pool(name="results", bufs=PASSES))
+        results = ctx.enter_context(tc.tile_pool(name="results", bufs=5))
         flip_banks = ctx.enter_context(tc.psum_pool(name="flip_banks", bufs=4))
         acc_banks = ctx.enter_context(tc.psum_pool(name="acc_banks", bufs=4))
+        ctx.enter_context(tc.manual_schedule())
 
+        weight_tiles = []
+        for h in range(WEIGHT_LOADS):
+            wrows = loaded.tile([P, WEIGHT_RUN, D], BF16)
+            nc.sync.dma_start(
+                out=wrows[:],
+                in_=s_out_w[h * 256 : (h + 1) * 256, :].rearrange("(p j) k -> p j k", j=WEIGHT_RUN),
+            )
+            weight_tiles.append(wrows)
         grad_rows = grad_out.rearrange("b n k -> (b n) k")
         grad_tiles = []
-        weight_tiles = []
-        for source, tiles in ((grad_rows, grad_tiles), (s_out_w, weight_tiles)):
-            for r in range(ROW_TILES):
-                rows = loaded.tile([P, D], BF16)
-                nc.sync.dma_start(out=rows[:], in_=source[r * P : (r + 1) * P, :])
-                tiles.append(rows)
+        for r in range(GRAD_TILES):
+            grows = loaded.tile([P, D], BF16)
+            nc.sync.dma_start(out=grows[:], in_=grad_rows[r * P : (r + 1) * P, :])
+            grad_tiles.append(grows)
 
         ident = consts.tile([P, P], F32)
         make_identity(nc, ident[:])
-        sorter = consts.tile([P, P], F32)
-        full = sorter[:, 0:FULL_SORTED].rearrange(
-            "k (i l t h) -> k i l t h", i=FULL_PASSES, l=TILE_SAMPLES, t=FRAMES, h=HALVES
-        )
-        token = ident[:].rearrange("k (l n) -> k l n", l=TILE_SAMPLES)
-        for h in range(HALVES):
-            first = FRAMES * (PASSES * h + 1) - (FRAMES - 1)
-            nc.vector.tensor_copy(
-                out=full[:, :, :, :, h],
-                in_=token[:, :, first : first + FULL_PASSES * FRAMES].rearrange("k l (i t) -> k i l t", t=FRAMES),
-            )
-        first = FRAMES * PASSES - (FRAMES - 1)
-        nc.vector.tensor_copy(
-            out=sorter[:, FULL_SORTED : FULL_SORTED + TILE_SEQUENCES].rearrange("k (l t) -> k l t", t=FRAMES),
-            in_=token[:, :, first : first + FRAMES],
-        )
-        nc.vector.tensor_copy(out=sorter[:, FULL_SORTED + TILE_SEQUENCES : P], in_=token[:, :, 0])
-
-        grad_grouped = operands.tile([P, PASSES * P * 4], BF16, align_bytes=64)
-        grad_codes = operands.tile([P, PASSES * P], U32, align_bytes=64)
-        grad_scales = operands.tile([P, PASSES * P], U8, align_bytes=64)
+        grad_grouped = operands.tile([P, COLS * 4], BF16, align_bytes=64)
+        grad_codes = operands.tile([P, COLS], U32, align_bytes=64)
+        grad_scales = operands.tile([P, COLS], U8, align_bytes=64)
         weight_grouped = operands.tile([P, D * 4], BF16, align_bytes=64)
         weight_codes = operands.tile([P, D], U32, align_bytes=64)
         weight_scales = operands.tile([P, D], U8, align_bytes=64)
-        grad_words = grad_grouped[:].bitcast(F32).rearrange(
-            "k (i q u) -> k i q u", i=PASSES, q=P, u=WORD_PLANES
+        grad_words = grad_grouped[:].bitcast(F32).rearrange("k (c u) -> k c u", u=WORDS)
+        weight_words = weight_grouped[:].bitcast(F32).rearrange("k (c u) -> k c u", u=WORDS)
+        nc.vector.memset(grad_grouped[:].bitcast(F32)[:, ROWS * WORDS : COLS * WORDS], 0.0)
+        sorter = consts.tile([P, P], F32)
+        by_sample = ident[:].rearrange("k (l n) -> k l n", l=TILE_SAMPLES)
+        nc.vector.tensor_copy(
+            out=sorter[:, 0:TILE_PATCHES].rearrange("k (l t s) -> k l t s", l=TILE_SAMPLES, t=FRAMES),
+            in_=by_sample[:, :, 1:TOKENS].rearrange("k l (s t) -> k l t s", t=FRAMES),
         )
-        weight_words = weight_grouped[:].bitcast(F32).rearrange("k (c u) -> k c u", u=WORD_PLANES)
-        nc.vector.memset(grad_grouped[:].bitcast(F32), 0.0)
-
-        for r in range(ROW_TILES):
-            words = grad_tiles[r][:].bitcast(F32)
-            flipped = flip_banks.tile([P, WORD_PLANES, BANK_WORDS // WORD_PLANES], F32)
-            for u in range(WORD_PLANES):
-                nc.tensor.transpose(flipped[:, u, 0:P], words[:, u : D // 2 : WORD_PLANES], sorter[:])
-            mine = grad_words[:, :, r * SLOTS : (r + 1) * SLOTS, :]
-            moves = (
-                (
-                    mine[:, 1:PASSES, :, :],
-                    flipped[:, :, 0:FULL_SORTED].rearrange("k u (i c) -> k i c u", i=FULL_PASSES),
-                ),
-                (
-                    mine[:, 0, 1:SLOTS:HALVES, :],
-                    flipped[:, :, FULL_SORTED : FULL_SORTED + TILE_SEQUENCES].rearrange("k u c -> k c u"),
-                ),
-                (
-                    mine[:, 0, 0 : SLOTS : FRAMES * HALVES, :],
-                    flipped[:, :, FULL_SORTED + TILE_SEQUENCES : P].rearrange("k u c -> k c u"),
-                ),
+        nc.vector.tensor_copy(out=sorter[:, TILE_PATCHES:P], in_=by_sample[:, :, 0])
+        is_class = consts.tile([P, len(STARTS)], F32)
+        for i, start in enumerate(STARTS):
+            nc.vector.reduce_sum(
+                out=is_class[:, i : i + 1],
+                in_=ident[:, (-start) % POSITIONS : P : POSITIONS],
+                axis=mybir.AxisListType.X,
             )
-            for target, sorted_words in moves:
-                if r % 2 == 0:
-                    nc.vector.tensor_copy(out=target, in_=sorted_words)
-                else:
-                    nc.scalar.copy(out=target, in_=sorted_words)
-        for i in range(PASSES):
+        factor = consts.tile([P, len(STARTS)], F32)
+        nc.vector.tensor_scalar(
+            out=factor[:], in0=is_class[:], scalar1=1.0 / FRAMES - 1.0, scalar2=1.0, op0=MULT, op1=ADD
+        )
+
+        weight_flips = []
+        for h in range(WEIGHT_LOADS):
+            wwords = weight_tiles[h][:].rearrange("p j k -> p (j k)").bitcast(F32)
+            wflip = flip_banks.tile([P, WEIGHT_RUN, WORDS, P], F32, tag="flip")
+            for j in range(WEIGHT_RUN):
+                for u in range(WORDS):
+                    nc.tensor.transpose(
+                        wflip[:, j, u, :], wwords[:, j * D // 2 + u : (j + 1) * D // 2 : WORDS], ident[:]
+                    )
+            weight_flips.append(wflip)
+        grad_flips = []
+        for r in range(GRAD_TILES):
+            gwords = grad_tiles[r][:].bitcast(F32)
+            gflip = (flip_banks if r < 2 else acc_banks).tile([P, WORDS, P], F32, tag="flip" if r < 2 else "acc")
+            for u in range(WORDS):
+                nc.tensor.transpose(gflip[:, u, :], gwords[:, u : D // 2 : WORDS], sorter[:])
+            grad_flips.append(gflip)
+
+        def copy_weight(engine, h):
+            engine(
+                out=weight_words[:, h * 256 : (h + 1) * 256, :].rearrange("k (p j) u -> k p j u", j=WEIGHT_RUN),
+                in_=weight_flips[h][:].rearrange("k j u p -> k p j u"),
+            )
+
+        def copy_grad(engine, r):
+            mine = grad_words[:, r * TILE_ROWS : (r + 1) * TILE_ROWS, :].rearrange("k (j s) u -> k j s u", s=POSITIONS)
+            engine(
+                out=mine[:, :, 1:POSITIONS, :],
+                in_=grad_flips[r][:, :, 0:TILE_PATCHES].rearrange("k u (j s) -> k j s u", s=PATCHES),
+            )
+            engine(
+                out=mine[:, :, 0, :].rearrange("k (l t) u -> k l t u", t=FRAMES),
+                in_=grad_flips[r][:, :, TILE_PATCHES:P]
+                .rearrange("k u l -> k l u")
+                .unsqueeze(2)
+                .to_broadcast([P, TILE_SAMPLES, FRAMES, WORDS]),
+            )
+
+        def quantise_weight(h):
             nc.vector.quantize_mx(
-                out=grad_codes[:, i * P : (i + 1) * P].bitcast(E5M2_X4),
-                scales=grad_scales[:, i * P : (i + 1) * P],
-                in_=grad_grouped[:, i * P * 4 : (i + 1) * P * 4],
+                out=weight_codes[:, h * 256 : (h + 1) * 256].bitcast(E4M3_X4),
+                scales=weight_scales[:, h * 256 : (h + 1) * 256],
+                in_=weight_grouped[:, h * 1024 : (h + 1) * 1024],
             )
 
-        for r in range(ROW_TILES):
-            words = weight_tiles[r][:].bitcast(F32)
-            flipped = flip_banks.tile([P, WORD_PLANES, BANK_WORDS // WORD_PLANES], F32)
-            for u in range(WORD_PLANES):
-                nc.tensor.transpose(flipped[:, u, 0:P], words[:, u : D // 2 : WORD_PLANES], ident[:])
-            nc.scalar.copy(
-                out=weight_words[:, r * P : (r + 1) * P, :],
-                in_=flipped[:, :, 0:P].rearrange("k u c -> k c u"),
-            )
+        def quantise_grad(first, last):
             nc.vector.quantize_mx(
-                out=weight_codes[:, r * P : (r + 1) * P].bitcast(E4M3_X4),
-                scales=weight_scales[:, r * P : (r + 1) * P],
-                in_=weight_grouped[:, r * P * 4 : (r + 1) * P * 4],
+                out=grad_codes[:, first:last].bitcast(E5M2_X4),
+                scales=grad_scales[:, first:last],
+                in_=grad_grouped[:, first * 4 : last * 4],
             )
 
-        out_rows = out.rearrange("j s d -> (j s) d").rearrange("(q i) d -> q i d", i=PASSES)
-        class_rows_of_out = out.rearrange("(b t) s d -> b t s d", t=FRAMES)[:, :, 0, :]
-        for i in range(PASSES):
-            acc = acc_banks.tile([P, D], F32)
+        accs = {}
+
+        def multiply(i):
+            acc = acc_banks.tile([P, D], F32, tag="acc")
+            accs[i] = acc
+            cols = slice(STARTS[i], STARTS[i] + P)
             nc.tensor.matmul_mx(
                 out=acc[:],
-                lhsT=grad_codes[:, i * P : (i + 1) * P].bitcast(E5M2_X4),
-                lhsT_scale=grad_scales[:, i * P : (i + 1) * P],
+                lhsT=grad_codes[:, cols].bitcast(E5M2_X4),
+                lhsT_scale=grad_scales[:, cols],
                 rhs=weight_codes[:].bitcast(E4M3_X4),
                 rhs_scale=weight_scales[:],
                 start=True,
                 stop=True,
             )
+
+        def finish(i, on_vector):
             result = results.tile([P, D], F32)
-            if i == 0:
-                nc.vector.tensor_copy(out=result[:], in_=acc[:])
-                nc.sync.dma_start(out=out[:, PASSES, :], in_=result[1:USED:HALVES, :])
-                class_result = results.tile([P, D], F32)
-                nc.vector.tensor_scalar_mul(out=class_result[:], in0=acc[:], scalar1=1.0 / FRAMES)
-                nc.sync.dma_start(
-                    out=class_rows_of_out,
-                    in_=class_result[0 : USED : FRAMES * HALVES, :]
-                    .unsqueeze(1)
-                    .to_broadcast([SAMPLES, FRAMES, D]),
-                )
-            elif i % 2 == 0:
-                nc.vector.tensor_copy(out=result[:], in_=acc[:])
-                nc.sync.dma_start(out=out_rows[:, i, :], in_=result[0:USED, :])
+            if on_vector:
+                nc.vector.tensor_scalar_mul(out=result[:], in0=accs[i][:], scalar1=factor[:, i : i + 1])
             else:
-                nc.scalar.copy(out=result[:], in_=acc[:])
-                nc.scalar.dma_start(out=out_rows[:, i, :], in_=result[0:USED, :])
+                nc.scalar.activation(out=result[:], in_=accs[i][:], func=COPY, scale=factor[:, i : i + 1])
+            rows = out.rearrange("j s d -> (j s) d")
+            if i < 4:
+                nc.sync.dma_start(out=rows[STARTS[i] : STARTS[i] + P, :], in_=result[:])
+            else:
+                nc.sync.dma_start(out=rows[512:544, :], in_=result[64:96, :])
+                nc.sync.dma_start(out=rows[544:560, :], in_=result[96:112, :])
+
+        copy_weight(nc.scalar.copy, 0)
+        copy_weight(nc.vector.tensor_copy, 1)
+        copy_grad(nc.scalar.copy, 0)
+        quantise_weight(0)
+        quantise_weight(1)
+        copy_grad(nc.scalar.copy, 1)
+        quantise_grad(0, 128)
+        multiply(0)
+        copy_grad(nc.scalar.copy, 2)
+        quantise_grad(128, 256)
+        multiply(1)
+        copy_grad(nc.scalar.copy, 3)
+        quantise_grad(256, 384)
+        multiply(2)
+        finish(0, False)
+        quantise_grad(384, 512)
+        quantise_grad(512, 576)
+        multiply(3)
+        finish(1, True)
+        finish(2, False)
+        multiply(4)
+        finish(3, True)
+        finish(4, False)

@@ -25,8 +25,7 @@ TILE_SAMPLES = P // TOKENS
 GRAD_TILES = 4
 TILE_ROWS = TILE_SAMPLES * FRAMES * POSITIONS
 TILE_PATCHES = TILE_SAMPLES * FRAMES * PATCHES
-WEIGHT_LOADS = 2
-WEIGHT_RUN = 2
+WEIGHT_TILES = 4
 WORDS = 2
 COLS = 576
 STARTS = (0, 128, 256, 384, 448)
@@ -39,27 +38,20 @@ def tile_timesformerlayer_pc_s_kernel(tc, ctx_s, x_res, s_out_w, s_out_b, grad_o
     nc = tc.nc
     with ExitStack() as ctx:
         consts = ctx.enter_context(tc.tile_pool(name="consts", bufs=1))
-        loaded = ctx.enter_context(tc.tile_pool(name="loaded", bufs=4))
+        loaded = ctx.enter_context(tc.tile_pool(name="loaded", bufs=8))
         operands = ctx.enter_context(tc.tile_pool(name="operands", bufs=1))
-        results = ctx.enter_context(tc.tile_pool(name="results", bufs=5))
-        flip_banks = ctx.enter_context(tc.psum_pool(name="flip_banks", bufs=4))
-        acc_banks = ctx.enter_context(tc.psum_pool(name="acc_banks", bufs=4))
+        results = ctx.enter_context(tc.tile_pool(name="results", bufs=6))
+        banks = ctx.enter_context(tc.psum_pool(name="banks", bufs=8))
         ctx.enter_context(tc.manual_schedule())
 
-        weight_tiles = []
-        for h in range(WEIGHT_LOADS):
-            wrows = loaded.tile([P, WEIGHT_RUN, D], BF16)
-            nc.sync.dma_start(
-                out=wrows[:],
-                in_=s_out_w[h * 256 : (h + 1) * 256, :].rearrange("(p j) k -> p j k", j=WEIGHT_RUN),
-            )
-            weight_tiles.append(wrows)
         grad_rows = grad_out.rearrange("b n k -> (b n) k")
-        grad_tiles = []
-        for r in range(GRAD_TILES):
-            grows = loaded.tile([P, D], BF16)
-            nc.sync.dma_start(out=grows[:], in_=grad_rows[r * P : (r + 1) * P, :])
-            grad_tiles.append(grows)
+        order = (("g", 0), ("w", 0), ("w", 1), ("w", 2), ("w", 3), ("g", 1), ("g", 2), ("g", 3))
+        loaded_tiles = {}
+        for kind, r in order:
+            rows_tile = loaded.tile([P, D], BF16, tag="rows")
+            source = s_out_w if kind == "w" else grad_rows
+            nc.sync.dma_start(out=rows_tile[:], in_=source[r * P : (r + 1) * P, :])
+            loaded_tiles[kind, r] = rows_tile
 
         ident = consts.tile([P, P], F32)
         make_identity(nc, ident[:])
@@ -91,49 +83,43 @@ def tile_timesformerlayer_pc_s_kernel(tc, ctx_s, x_res, s_out_w, s_out_b, grad_o
             out=factor[:], in0=is_class[:], scalar1=1.0 / FRAMES - 1.0, scalar2=1.0, op0=MULT, op1=ADD
         )
 
-        weight_flips = []
-        for h in range(WEIGHT_LOADS):
-            wwords = weight_tiles[h][:].rearrange("p j k -> p (j k)").bitcast(F32)
-            wflip = flip_banks.tile([P, WEIGHT_RUN, WORDS, P], F32, tag="flip")
-            for j in range(WEIGHT_RUN):
-                for u in range(WORDS):
-                    nc.tensor.transpose(
-                        wflip[:, j, u, :], wwords[:, j * D // 2 + u : (j + 1) * D // 2 : WORDS], ident[:]
-                    )
-            weight_flips.append(wflip)
-        grad_flips = []
-        for r in range(GRAD_TILES):
-            gwords = grad_tiles[r][:].bitcast(F32)
-            gflip = (flip_banks if r < 2 else acc_banks).tile([P, WORDS, P], F32, tag="flip" if r < 2 else "acc")
-            for u in range(WORDS):
-                nc.tensor.transpose(gflip[:, u, :], gwords[:, u : D // 2 : WORDS], sorter[:])
-            grad_flips.append(gflip)
+        flips = {}
 
-        def copy_weight(engine, h):
+        def flip(kind, r):
+            words = loaded_tiles[kind, r][:].bitcast(F32)
+            flipped = banks.tile([P, WORDS, P], F32, tag="bank")
+            for u in range(WORDS):
+                nc.tensor.transpose(
+                    flipped[:, u, :], words[:, u : D // 2 : WORDS], ident[:] if kind == "w" else sorter[:]
+                )
+            flips[kind, r] = flipped
+
+        def copy_weight(engine, r):
             engine(
-                out=weight_words[:, h * 256 : (h + 1) * 256, :].rearrange("k (p j) u -> k p j u", j=WEIGHT_RUN),
-                in_=weight_flips[h][:].rearrange("k j u p -> k p j u"),
+                out=weight_words[:, r * P : (r + 1) * P, :],
+                in_=flips["w", r][:].rearrange("k u c -> k c u"),
             )
 
         def copy_grad(engine, r):
             mine = grad_words[:, r * TILE_ROWS : (r + 1) * TILE_ROWS, :].rearrange("k (j s) u -> k j s u", s=POSITIONS)
             engine(
                 out=mine[:, :, 1:POSITIONS, :],
-                in_=grad_flips[r][:, :, 0:TILE_PATCHES].rearrange("k u (j s) -> k j s u", s=PATCHES),
+                in_=flips["g", r][:, :, 0:TILE_PATCHES].rearrange("k u (j s) -> k j s u", s=PATCHES),
             )
             engine(
                 out=mine[:, :, 0, :].rearrange("k (l t) u -> k l t u", t=FRAMES),
-                in_=grad_flips[r][:, :, TILE_PATCHES:P]
+                in_=flips["g", r][:, :, TILE_PATCHES:P]
                 .rearrange("k u l -> k l u")
                 .unsqueeze(2)
                 .to_broadcast([P, TILE_SAMPLES, FRAMES, WORDS]),
             )
 
-        def quantise_weight(h):
+        def quantise_weight(r):
+            cols = slice(r * P, (r + 1) * P)
             nc.vector.quantize_mx(
-                out=weight_codes[:, h * 256 : (h + 1) * 256].bitcast(E4M3_X4),
-                scales=weight_scales[:, h * 256 : (h + 1) * 256],
-                in_=weight_grouped[:, h * 1024 : (h + 1) * 1024],
+                out=weight_codes[:, cols].bitcast(E4M3_X4),
+                scales=weight_scales[:, cols],
+                in_=weight_grouped[:, r * P * 4 : (r + 1) * P * 4],
             )
 
         def quantise_grad(first, last):
@@ -146,7 +132,7 @@ def tile_timesformerlayer_pc_s_kernel(tc, ctx_s, x_res, s_out_w, s_out_b, grad_o
         accs = {}
 
         def multiply(i):
-            acc = acc_banks.tile([P, D], F32, tag="acc")
+            acc = banks.tile([P, D], F32, tag="bank")
             accs[i] = acc
             cols = slice(STARTS[i], STARTS[i] + P)
             nc.tensor.matmul_mx(
@@ -159,39 +145,43 @@ def tile_timesformerlayer_pc_s_kernel(tc, ctx_s, x_res, s_out_w, s_out_b, grad_o
                 stop=True,
             )
 
+        rows_of_out = out.rearrange("j s d -> (j s) d")
+
         def finish(i, on_vector):
-            result = results.tile([P, D], F32)
+            result = results.tile([P, D], F32, tag="result")
             if on_vector:
                 nc.vector.tensor_scalar_mul(out=result[:], in0=accs[i][:], scalar1=factor[:, i : i + 1])
             else:
                 nc.scalar.activation(out=result[:], in_=accs[i][:], func=COPY, scale=factor[:, i : i + 1])
-            rows = out.rearrange("j s d -> (j s) d")
             if i < 4:
-                nc.sync.dma_start(out=rows[STARTS[i] : STARTS[i] + P, :], in_=result[:])
+                nc.sync.dma_start(out=rows_of_out[STARTS[i] : STARTS[i] + P, :], in_=result[:])
             else:
-                nc.sync.dma_start(out=rows[512:544, :], in_=result[64:96, :])
-                nc.sync.dma_start(out=rows[544:560, :], in_=result[96:112, :])
+                nc.sync.dma_start(out=rows_of_out[512:544, :], in_=result[64:96, :])
+                nc.sync.dma_start(out=rows_of_out[544:560, :], in_=result[96:112, :])
 
+        for kind, r in order:
+            flip(kind, r)
+        copy_grad(nc.vector.tensor_copy, 0)
         copy_weight(nc.scalar.copy, 0)
-        copy_weight(nc.vector.tensor_copy, 1)
-        copy_grad(nc.scalar.copy, 0)
         quantise_weight(0)
-        quantise_weight(1)
-        copy_grad(nc.scalar.copy, 1)
         quantise_grad(0, 128)
+        for r in range(1, WEIGHT_TILES):
+            copy_weight(nc.scalar.copy, r)
+            quantise_weight(r)
         multiply(0)
-        copy_grad(nc.scalar.copy, 2)
+        copy_grad(nc.scalar.copy, 1)
         quantise_grad(128, 256)
         multiply(1)
-        copy_grad(nc.scalar.copy, 3)
+        finish(0, True)
+        copy_grad(nc.scalar.copy, 2)
         quantise_grad(256, 384)
         multiply(2)
-        finish(0, False)
+        copy_grad(nc.scalar.copy, 3)
         quantise_grad(384, 512)
-        quantise_grad(512, 576)
         multiply(3)
-        finish(1, True)
-        finish(2, False)
+        quantise_grad(512, 576)
         multiply(4)
-        finish(3, True)
-        finish(4, False)
+        finish(1, False)
+        finish(2, True)
+        finish(3, False)
+        finish(4, True)

@@ -53,6 +53,8 @@ def tile_timesformerlayer_pc_s_kernel(tc, ctx_s, x_res, s_out_w, s_out_b, grad_o
             nc.sync.dma_start(out=rows_tile[:], in_=source[r * P : (r + 1) * P, :])
             loaded_tiles[kind, r] = rows_tile
 
+        zeros = consts.tile([P, D], F32)
+        nc.vector.memset(zeros[:], 0.0)
         ident = consts.tile([P, P], F32)
         make_identity(nc, ident[:])
         grad_grouped = operands.tile([P, COLS * 4], BF16, align_bytes=64)
@@ -158,6 +160,9 @@ def tile_timesformerlayer_pc_s_kernel(tc, ctx_s, x_res, s_out_w, s_out_b, grad_o
             else:
                 nc.sync.dma_start(out=rows_of_out[512:544, :], in_=result[64:96, :])
                 nc.sync.dma_start(out=rows_of_out[544:560, :], in_=result[96:112, :])
+
+        idle_acc = banks.tile([P, D], F32, tag="bank")
+        nc.tensor.matmul(idle_acc[:], lhsT=zeros[:, 0:P], rhs=zeros[:], start=True, stop=True)
 
         for kind, r in order:
             flip(kind, r)

@@ -53,7 +53,7 @@ def tile_timesformerlayer_pc_s_kernel(tc, ctx_s, x_res, s_out_w, s_out_b, grad_o
             nc.sync.dma_start(out=rows_tile[:], in_=source[r * P : (r + 1) * P, :])
             loaded_tiles[kind, r] = rows_tile
 
-        zeros = consts.tile([P, D], F32)
+        zeros = consts.tile([P, P], F32)
         nc.vector.memset(zeros[:], 0.0)
         ident = consts.tile([P, P], F32)
         make_identity(nc, ident[:])
@@ -161,8 +161,8 @@ def tile_timesformerlayer_pc_s_kernel(tc, ctx_s, x_res, s_out_w, s_out_b, grad_o
                 nc.sync.dma_start(out=rows_of_out[512:544, :], in_=result[64:96, :])
                 nc.sync.dma_start(out=rows_of_out[544:560, :], in_=result[96:112, :])
 
-        idle_acc = banks.tile([P, D], F32, tag="bank")
-        nc.tensor.matmul(idle_acc[:], lhsT=zeros[:, 0:P], rhs=zeros[:], start=True, stop=True)
+        idle_acc = banks.tile([P, 4, P], F32, tag="bank")
+        nc.tensor.matmul(idle_acc[:], lhsT=zeros[:], rhs=zeros[:].unsqueeze(1).to_broadcast([P, 4, P]), start=True, stop=True)
 
         for kind, r in order:
             flip(kind, r)
@@ -177,16 +177,16 @@ def tile_timesformerlayer_pc_s_kernel(tc, ctx_s, x_res, s_out_w, s_out_b, grad_o
         copy_grad(nc.scalar.copy, 1)
         quantise_grad(128, 256)
         multiply(1)
-        finish(0, True)
         copy_grad(nc.scalar.copy, 2)
         quantise_grad(256, 384)
         multiply(2)
+        finish(0, True)
         copy_grad(nc.scalar.copy, 3)
         quantise_grad(384, 512)
         multiply(3)
         quantise_grad(512, 576)
         multiply(4)
         finish(1, False)
-        finish(2, True)
-        finish(3, False)
-        finish(4, True)
+        finish(2, False)
+        finish(3, True)
+        finish(4, False)

@@ -28,6 +28,7 @@ TILE_PATCHES = TILE_SAMPLES * FRAMES * PATCHES
 WEIGHT_TILES = 4
 WORDS = 2
 COLS = 576
+HALF = D // 2
 STARTS = (0, 128, 256, 384, 448)
 
 FLOPS = 2 * SAMPLES * TOKENS * D * D
@@ -61,11 +62,13 @@ def tile_timesformerlayer_pc_s_kernel(tc, ctx_s, x_res, s_out_w, s_out_b, grad_o
         grad_codes = operands.tile([P, COLS], U32, align_bytes=64)
         grad_scales = operands.tile([P, COLS], U8, align_bytes=64)
         weight_grouped = operands.tile([P, D * 4], BF16, align_bytes=64)
-        weight_codes = operands.tile([P, D], U32, align_bytes=64)
-        weight_scales = operands.tile([P, D], U8, align_bytes=64)
+        weight_codes = operands.tile([P, HALF + D], U32, align_bytes=64)
+        weight_scales = operands.tile([P, HALF + D], U8, align_bytes=64)
         grad_words = grad_grouped[:].bitcast(F32).rearrange("k (c u) -> k c u", u=WORDS)
         weight_words = weight_grouped[:].bitcast(F32).rearrange("k (c u) -> k c u", u=WORDS)
         nc.vector.memset(grad_grouped[:].bitcast(F32)[:, ROWS * WORDS : COLS * WORDS], 0.0)
+        nc.vector.memset(weight_codes[:, 0:HALF], 0)
+        nc.vector.memset(weight_scales[:, 0:HALF].bitcast(U32), 0)
         sorter = consts.tile([P, P], F32)
         by_sample = ident[:].rearrange("k (l n) -> k l n", l=TILE_SAMPLES)
         nc.vector.tensor_copy(
@@ -117,7 +120,7 @@ def tile_timesformerlayer_pc_s_kernel(tc, ctx_s, x_res, s_out_w, s_out_b, grad_o
             )
 
         def quantise_weight(r):
-            cols = slice(r * P, (r + 1) * P)
+            cols = slice(HALF + r * P, HALF + (r + 1) * P)
             nc.vector.quantize_mx(
                 out=weight_codes[:, cols].bitcast(E4M3_X4),
                 scales=weight_scales[:, cols],
@@ -133,30 +136,31 @@ def tile_timesformerlayer_pc_s_kernel(tc, ctx_s, x_res, s_out_w, s_out_b, grad_o
 
         accs = {}
 
-        def multiply(i):
+        def multiply(i, window=HALF):
             acc = banks.tile([P, D], F32, tag="bank")
-            accs[i] = acc
+            accs[i, window] = acc
             cols = slice(STARTS[i], STARTS[i] + P)
             nc.tensor.matmul_mx(
                 out=acc[:],
                 lhsT=grad_codes[:, cols].bitcast(E5M2_X4),
                 lhsT_scale=grad_scales[:, cols],
-                rhs=weight_codes[:].bitcast(E4M3_X4),
-                rhs_scale=weight_scales[:],
+                rhs=weight_codes[:, window : window + D].bitcast(E4M3_X4),
+                rhs_scale=weight_scales[:, window : window + D],
                 start=True,
                 stop=True,
             )
 
         rows_of_out = out.rearrange("j s d -> (j s) d")
 
-        def finish(i, on_vector):
-            result = results.tile([P, D], F32, tag="result")
+        def finish(i, on_vector, window=HALF, first=0, last=D):
+            result = results.tile([P, last - first], F32, tag="result")
+            source = accs[i, window][:, first + HALF - window : last + HALF - window]
             if on_vector:
-                nc.vector.tensor_scalar_mul(out=result[:], in0=accs[i][:], scalar1=factor[:, i : i + 1])
+                nc.vector.tensor_scalar_mul(out=result[:], in0=source, scalar1=factor[:, i : i + 1])
             else:
-                nc.scalar.activation(out=result[:], in_=accs[i][:], func=COPY, scale=factor[:, i : i + 1])
+                nc.scalar.activation(out=result[:], in_=source, func=COPY, scale=factor[:, i : i + 1])
             if i < 4:
-                nc.sync.dma_start(out=rows_of_out[STARTS[i] : STARTS[i] + P, :], in_=result[:])
+                nc.sync.dma_start(out=rows_of_out[STARTS[i] : STARTS[i] + P, first:last], in_=result[:])
             else:
                 nc.sync.dma_start(out=rows_of_out[512:544, :], in_=result[64:96, :])
                 nc.sync.dma_start(out=rows_of_out[544:560, :], in_=result[96:112, :])
@@ -170,17 +174,22 @@ def tile_timesformerlayer_pc_s_kernel(tc, ctx_s, x_res, s_out_w, s_out_b, grad_o
         copy_weight(nc.scalar.copy, 0)
         quantise_weight(0)
         quantise_grad(0, 128)
-        for r in range(1, WEIGHT_TILES):
-            copy_weight(nc.scalar.copy, r)
-            quantise_weight(r)
+        copy_weight(nc.scalar.copy, 1)
+        quantise_weight(1)
+        multiply(0, 0)
+        copy_weight(nc.scalar.copy, 2)
+        quantise_weight(2)
+        copy_weight(nc.scalar.copy, 3)
+        quantise_weight(3)
         multiply(0)
         copy_grad(nc.scalar.copy, 1)
         quantise_grad(128, 256)
         multiply(1)
+        finish(0, True, 0, 0, HALF)
         copy_grad(nc.scalar.copy, 2)
         quantise_grad(256, 384)
         multiply(2)
-        finish(0, True)
+        finish(0, True, HALF, HALF, D)
         copy_grad(nc.scalar.copy, 3)
         quantise_grad(384, 512)
         multiply(3)

@@ -41,7 +41,7 @@ def tile_timesformerlayer_pc_s_kernel(tc, ctx_s, x_res, s_out_w, s_out_b, grad_o
         consts = ctx.enter_context(tc.tile_pool(name="consts", bufs=1))
         loaded = ctx.enter_context(tc.tile_pool(name="loaded", bufs=8))
         operands = ctx.enter_context(tc.tile_pool(name="operands", bufs=1))
-        results = ctx.enter_context(tc.tile_pool(name="results", bufs=6))
+        results = ctx.enter_context(tc.tile_pool(name="results", bufs=7))
         banks = ctx.enter_context(tc.psum_pool(name="banks", bufs=8))
         ctx.enter_context(tc.manual_schedule())
 
@@ -165,8 +165,13 @@ def tile_timesformerlayer_pc_s_kernel(tc, ctx_s, x_res, s_out_w, s_out_b, grad_o
                 nc.sync.dma_start(out=rows_of_out[512:544, :], in_=result[64:96, :])
                 nc.sync.dma_start(out=rows_of_out[544:560, :], in_=result[96:112, :])
 
-        idle_acc = banks.tile([P, 4, P], F32, tag="bank")
-        nc.tensor.matmul(idle_acc[:], lhsT=zeros[:], rhs=zeros[:].unsqueeze(1).to_broadcast([P, 4, P]), start=True, stop=True)
+        short_zeros = zeros[:].bitcast(BF16)
+        idle_acc = banks.tile([P, 2, P], F32, tag="bank")
+        nc.tensor.matmul(idle_acc[:], lhsT=short_zeros[:, 0:P], rhs=short_zeros, start=True, stop=True)
+        idle_acc2 = banks.tile([P, 4, P], F32, tag="bank")
+        nc.tensor.matmul(
+            idle_acc2[:], lhsT=zeros[:], rhs=zeros[:].unsqueeze(1).to_broadcast([P, 4, P]), start=True, stop=True
+        )
 
         for kind, r in order:
             flip(kind, r)
@@ -189,13 +194,14 @@ def tile_timesformerlayer_pc_s_kernel(tc, ctx_s, x_res, s_out_w, s_out_b, grad_o
         copy_grad(nc.scalar.copy, 2)
         quantise_grad(256, 384)
         multiply(2)
-        finish(0, True, HALF, HALF, D)
         copy_grad(nc.scalar.copy, 3)
+        finish(0, False, HALF, HALF, D)
         quantise_grad(384, 512)
         multiply(3)
         quantise_grad(512, 576)
         multiply(4)
-        finish(1, False)
-        finish(2, False)
-        finish(3, True)
-        finish(4, False)
+        finish(1, False, HALF, 0, HALF)
+        finish(1, False, HALF, HALF, D)
+        finish(2, True)
+        finish(3, False)
+        finish(4, True)

from contextlib import ExitStack

import concourse.mybir as mybir
from concourse.masks import make_identity

BF16 = mybir.dt.bfloat16
F32 = mybir.dt.float32
U32 = mybir.dt.uint32
U8 = mybir.dt.uint8
E5M2_X4 = mybir.dt.float8_e5m2_x4
E4M3_X4 = mybir.dt.float8_e4m3fn_x4
ADD = mybir.AluOpType.add
MULT = mybir.AluOpType.mult
COPY = mybir.ActivationFunctionType.Copy

P = 128
SAMPLES = 8
FRAMES = 7
POSITIONS = 10
PATCHES = 9
TOKENS = 64
D = 512
ROWS = SAMPLES * FRAMES * POSITIONS
TILE_SAMPLES = P // TOKENS
GRAD_TILES = 4
TILE_ROWS = TILE_SAMPLES * FRAMES * POSITIONS
TILE_PATCHES = TILE_SAMPLES * FRAMES * PATCHES
WEIGHT_TILES = 4
WORDS = 2
COLS = 576
HALF = D // 2
STARTS = (0, 128, 256, 384, 448)

FLOPS = 2 * SAMPLES * TOKENS * D * D
BYTES = 2 * (SAMPLES * TOKENS * D + D * D) + 4 * ROWS * D


def tile_timesformerlayer_pc_s_kernel(tc, ctx_s, x_res, s_out_w, s_out_b, grad_out, out):
    nc = tc.nc
    with ExitStack() as ctx:
        consts = ctx.enter_context(tc.tile_pool(name="consts", bufs=1))
        loaded = ctx.enter_context(tc.tile_pool(name="loaded", bufs=8))
        operands = ctx.enter_context(tc.tile_pool(name="operands", bufs=1))
        results = ctx.enter_context(tc.tile_pool(name="results", bufs=7))
        banks = ctx.enter_context(tc.psum_pool(name="banks", bufs=8))
        ctx.enter_context(tc.manual_schedule())

        grad_rows = grad_out.rearrange("b n k -> (b n) k")
        order = (("g", 0), ("w", 0), ("w", 1), ("w", 2), ("w", 3), ("g", 1), ("g", 2), ("g", 3))
        loaded_tiles = {}
        for kind, r in order:
            rows_tile = loaded.tile([P, D], BF16, tag="rows")
            source = s_out_w if kind == "w" else grad_rows
            nc.sync.dma_start(out=rows_tile[:], in_=source[r * P : (r + 1) * P, :])
            loaded_tiles[kind, r] = rows_tile

        zeros = consts.tile([P, P], F32)
        nc.vector.memset(zeros[:], 0.0)
        ident = consts.tile([P, P], F32)
        make_identity(nc, ident[:])
        grad_grouped = operands.tile([P, COLS * 4], BF16, align_bytes=64)
        grad_codes = operands.tile([P, COLS], U32, align_bytes=64)
        grad_scales = operands.tile([P, COLS], U8, align_bytes=64)
        weight_grouped = operands.tile([P, D * 4], BF16, align_bytes=64)
        weight_codes = operands.tile([P, HALF + D], U32, align_bytes=64)
        weight_scales = operands.tile([P, HALF + D], U8, align_bytes=64)
        grad_words = grad_grouped[:].bitcast(F32).rearrange("k (c u) -> k c u", u=WORDS)
        weight_words = weight_grouped[:].bitcast(F32).rearrange("k (c u) -> k c u", u=WORDS)
        nc.vector.memset(grad_grouped[:].bitcast(F32)[:, ROWS * WORDS : COLS * WORDS], 0.0)
        nc.vector.memset(weight_codes[:, 0:HALF], 0)
        nc.vector.memset(weight_scales[:, 0:HALF].bitcast(U32), 0)
        sorter = consts.tile([P, P], F32)
        by_sample = ident[:].rearrange("k (l n) -> k l n", l=TILE_SAMPLES)
        nc.vector.tensor_copy(
            out=sorter[:, 0:TILE_PATCHES].rearrange("k (l t s) -> k l t s", l=TILE_SAMPLES, t=FRAMES),
            in_=by_sample[:, :, 1:TOKENS].rearrange("k l (s t) -> k l t s", t=FRAMES),
        )
        nc.vector.tensor_copy(out=sorter[:, TILE_PATCHES:P], in_=by_sample[:, :, 0])
        is_class = consts.tile([P, len(STARTS)], F32)
        for i, start in enumerate(STARTS):
            nc.vector.reduce_sum(
                out=is_class[:, i : i + 1],
                in_=ident[:, (-start) % POSITIONS : P : POSITIONS],
                axis=mybir.AxisListType.X,
            )
        factor = consts.tile([P, len(STARTS)], F32)
        nc.vector.tensor_scalar(
            out=factor[:], in0=is_class[:], scalar1=1.0 / FRAMES - 1.0, scalar2=1.0, op0=MULT, op1=ADD
        )

        flips = {}

        def flip(kind, r):
            words = loaded_tiles[kind, r][:].bitcast(F32)
            flipped = banks.tile([P, WORDS, P], F32, tag="bank")
            for u in range(WORDS):
                nc.tensor.transpose(
                    flipped[:, u, :], words[:, u : D // 2 : WORDS], ident[:] if kind == "w" else sorter[:]
                )
            flips[kind, r] = flipped

        def copy_weight(engine, r):
            engine(
                out=weight_words[:, r * P : (r + 1) * P, :],
                in_=flips["w", r][:].rearrange("k u c -> k c u"),
            )

        def copy_grad(engine, r):
            mine = grad_words[:, r * TILE_ROWS : (r + 1) * TILE_ROWS, :].rearrange("k (j s) u -> k j s u", s=POSITIONS)
            engine(
                out=mine[:, :, 1:POSITIONS, :],
                in_=flips["g", r][:, :, 0:TILE_PATCHES].rearrange("k u (j s) -> k j s u", s=PATCHES),
            )
            engine(
                out=mine[:, :, 0, :].rearrange("k (l t) u -> k l t u", t=FRAMES),
                in_=flips["g", r][:, :, TILE_PATCHES:P]
                .rearrange("k u l -> k l u")
                .unsqueeze(2)
                .to_broadcast([P, TILE_SAMPLES, FRAMES, WORDS]),
            )

        def quantise_weight(r):
            cols = slice(HALF + r * P, HALF + (r + 1) * P)
            nc.vector.quantize_mx(
                out=weight_codes[:, cols].bitcast(E4M3_X4),
                scales=weight_scales[:, cols],
                in_=weight_grouped[:, r * P * 4 : (r + 1) * P * 4],
            )

        def quantise_grad(first, last):
            nc.vector.quantize_mx(
                out=grad_codes[:, first:last].bitcast(E5M2_X4),
                scales=grad_scales[:, first:last],
                in_=grad_grouped[:, first * 4 : last * 4],
            )

        accs = {}

        def multiply(i, window=HALF):
            acc = banks.tile([P, D], F32, tag="bank")
            accs[i, window] = acc
            cols = slice(STARTS[i], STARTS[i] + P)
            nc.tensor.matmul_mx(
                out=acc[:],
                lhsT=grad_codes[:, cols].bitcast(E5M2_X4),
                lhsT_scale=grad_scales[:, cols],
                rhs=weight_codes[:, window : window + D].bitcast(E4M3_X4),
                rhs_scale=weight_scales[:, window : window + D],
                start=True,
                stop=True,
            )

        rows_of_out = out.rearrange("j s d -> (j s) d")

        def finish(i, on_vector, window=HALF, first=0, last=D):
            result = results.tile([P, last - first], F32, tag="result")
            source = accs[i, window][:, first + HALF - window : last + HALF - window]
            if on_vector:
                nc.vector.tensor_scalar_mul(out=result[:], in0=source, scalar1=factor[:, i : i + 1])
            else:
                nc.scalar.activation(out=result[:], in_=source, func=COPY, scale=factor[:, i : i + 1])
            if i < 4:
                nc.sync.dma_start(out=rows_of_out[STARTS[i] : STARTS[i] + P, first:last], in_=result[:])
            else:
                nc.sync.dma_start(out=rows_of_out[512:544, :], in_=result[64:96, :])
                nc.sync.dma_start(out=rows_of_out[544:560, :], in_=result[96:112, :])

        short_zeros = zeros[:].bitcast(BF16)
        idle_acc = banks.tile([P, 2, P], F32, tag="bank")
        nc.tensor.matmul(idle_acc[:], lhsT=short_zeros[:, 0:P], rhs=short_zeros, start=True, stop=True)
        idle_acc2 = banks.tile([P, 4, P], F32, tag="bank")
        nc.tensor.matmul(
            idle_acc2[:], lhsT=zeros[:], rhs=zeros[:].unsqueeze(1).to_broadcast([P, 4, P]), start=True, stop=True
        )

        for kind, r in order:
            flip(kind, r)
        copy_grad(nc.vector.tensor_copy, 0)
        copy_weight(nc.scalar.copy, 0)
        quantise_weight(0)
        quantise_grad(0, 128)
        copy_weight(nc.scalar.copy, 1)
        quantise_weight(1)
        multiply(0, 0)
        copy_weight(nc.scalar.copy, 2)
        quantise_weight(2)
        copy_weight(nc.scalar.copy, 3)
        quantise_weight(3)
        multiply(0)
        copy_grad(nc.scalar.copy, 1)
        quantise_grad(128, 256)
        multiply(1)
        finish(0, True, 0, 0, HALF)
        copy_grad(nc.scalar.copy, 2)
        quantise_grad(256, 384)
        multiply(2)
        copy_grad(nc.scalar.copy, 3)
        finish(0, False, HALF, HALF, D)
        quantise_grad(384, 512)
        multiply(3)
        quantise_grad(512, 576)
        multiply(4)
        finish(1, False, HALF, 0, HALF)
        finish(1, False, HALF, HALF, D)
        finish(2, True)
        finish(3, False)
        finish(4, True)
